import numpy as np
import ml_dtypes


def mxq(x, axis, fmt="e4m3"):
    dtype, down = {"e4m3": (ml_dtypes.float8_e4m3fn, 7), "e5m2": (ml_dtypes.float8_e5m2, 14)}[fmt]
    v = np.moveaxis(np.asarray(x, np.float32).astype(ml_dtypes.bfloat16).astype(np.float64), axis, -1)
    blocks = v.reshape(v.shape[:-1] + (-1, 32))
    amax = np.abs(blocks).max(-1, keepdims=True)
    byte = np.maximum(np.where(amax > 0, np.frexp(amax)[1] - 1 + 127, 0) - down, 1)
    scale = np.exp2(byte - 127.0)
    codes = (blocks / scale).astype(np.float32).astype(dtype).astype(np.float64)
    return np.moveaxis((codes * scale).reshape(v.shape), -1, axis)


WIDE = False


def mx_kscale(k):
    if not WIDE:
        return np.ones(k)
    levels = np.array([10, -10, 5, -5, 0])
    a = np.random.permutation(np.resize(levels, k // 512 * 4)).reshape(k // 512, 4)
    idx = np.arange(k)
    return np.exp2(a[idx // 512, idx % 128 // 32])


BF16 = ml_dtypes.bfloat16


def bf(x):
    return np.asarray(x, np.float32).astype(BF16)


def f64(x):
    return np.asarray(x).astype(np.float64)


BS, H, XDIM = 256, 128, 16128
IN = XDIM + 2 * H


def sigmoid(v):
    return 1.0 / (1.0 + np.exp(-v))


def setup_inputs():
    s = mx_kscale(IN)
    c = 1.0 / np.sqrt(IN)

    def draw_w():
        return bf(np.random.standard_normal((H, IN)) * c / s[None, :])

    def draw_b():
        return bf(np.random.standard_normal(H) * 0.3)

    return {
        "input_x": bf(np.random.standard_normal((BS, XDIM)) * s[:XDIM]),
        "previous_time": bf(np.random.standard_normal((BS, H)) * s[XDIM:XDIM + H]),
        "previous_layer": bf(np.random.standard_normal((BS, H)) * s[XDIM + H:]),
        "old_state": bf(np.random.standard_normal((BS, H)) * 0.5),
        "Wi": draw_w(), "bi": draw_b(),
        "Wf": draw_w(), "bf": draw_b(),
        "Wo": draw_w(), "bo": draw_b(),
        "Ws": draw_w(), "bs_state": draw_b(),
    }


def reference(input_x, previous_time, previous_layer, old_state, Wi, bi, Wf, bf, Wo, bo, Ws, bs_state):
    z = np.concatenate([f64(input_x), f64(previous_time), f64(previous_layer)], axis=1)
    W_all = np.concatenate([f64(Wi), f64(Wf), f64(Wo), f64(Ws)], axis=0)
    b_all = np.concatenate([f64(bi), f64(bf), f64(bo), f64(bs_state)], axis=0)
    proj = (mxq(z, 1, "e4m3") @ mxq(W_all, 1, "e4m3").T) + b_all
    gi, gf, go, gs = np.split(proj, 4, axis=1)
    input_gate = sigmoid(gi)
    forget_gate = sigmoid(gf)
    output_gate = sigmoid(go)
    new_state = forget_gate * f64(old_state) + input_gate * np.tanh(gs)
    new_hidden = output_gate * np.tanh(new_state)
    return new_hidden

@@ -1,0 +1,216 @@
+from contextlib import ExitStack
+
+import concourse.mybir as mybir
+from concourse.masks import make_identity
+
+BF16 = mybir.dt.bfloat16
+F32 = mybir.dt.float32
+U32 = mybir.dt.uint32
+U8 = mybir.dt.uint8
+FP8X4 = mybir.dt.float8_e4m3fn_x4
+ACT = mybir.ActivationFunctionType
+ALU = mybir.AluOpType
+
+P = 128
+BATCH = 256
+BATCH_TILES = BATCH // P
+HIDDEN = 128
+K = 16384
+K_PASS = 512
+GATES = 4
+
+FLOPS = 2 * BATCH * GATES * HIDDEN * K
+
+UNIT_COLS = 4096
+UNIT_WORDS = UNIT_COLS // 2
+UNIT_CODES = UNIT_COLS // 4
+UNIT_BANKS = 4
+W_UNIT_K = UNIT_COLS
+Z_UNIT_K = UNIT_COLS // BATCH_TILES
+W_UNIT_PASSES = W_UNIT_K // K_PASS
+Z_UNIT_PASSES = Z_UNIT_K // K_PASS
+SETS = K // W_UNIT_K
+Z_UNITS_PER_SET = W_UNIT_K // Z_UNIT_K
+
+RAW_BUFS = 8
+VECTOR_BANK = UNIT_BANKS - 1
+
+
+def tile_rnn_unit_k_kernel(
+    tc, input_x, previous_time, previous_layer, old_state, Wi, bi, Wf, bf, Wo, bo, Ws, bs_state, out
+):
+    nc = tc.nc
+
+    weights = [Wi, Wf, Ws, Wo]
+    biases = [bi, bf, bs_state, bo]
+    GATE_I, GATE_F, GATE_S, GATE_O = 0, 1, 2, 3
+
+    z_parts = [
+        (input_x, 0),
+        (previous_time, input_x.shape[1]),
+        (previous_layer, input_x.shape[1] + previous_time.shape[1]),
+    ]
+
+    units = []
+    for s in range(SETS):
+        units.extend([(True, s, half) for half in range(Z_UNITS_PER_SET)])
+        units.extend([(False, s, gate) for gate in range(GATES)])
+    n_units = len(units)
+
+    with ExitStack() as stack:
+        const = stack.enter_context(tc.tile_pool(name="const", bufs=1))
+        raw_pool = stack.enter_context(tc.tile_pool(name="raw", bufs=RAW_BUFS))
+        grouped_pool = stack.enter_context(tc.tile_pool(name="grouped", bufs=3))
+        z_mx_pool = stack.enter_context(tc.tile_pool(name="z_mx", bufs=2 * Z_UNITS_PER_SET))
+        w_mx_pool = stack.enter_context(tc.tile_pool(name="w_mx", bufs=3))
+        cell = stack.enter_context(tc.tile_pool(name="cell", bufs=1))
+        acc_pool = stack.enter_context(tc.psum_pool(name="acc", bufs=1))
+        ring = stack.enter_context(tc.psum_pool(name="ring", bufs=UNIT_BANKS))
+        stack.enter_context(tc.manual_schedule())
+
+        raw_tiles = {}
+        grouped_tiles = {}
+        mx_tiles = {}
+
+        def load(n):
+            is_z, s, index = units[n]
+            raw = raw_pool.tile([P, UNIT_COLS], BF16)
+            raw_tiles[n] = raw
+            if not is_z:
+                nc.sync.dma_start(out=raw[:], in_=weights[index][:, s * W_UNIT_K : (s + 1) * W_UNIT_K])
+                return
+            first_k = s * W_UNIT_K + index * Z_UNIT_K
+            by_batch_tile = raw[:].rearrange("p (m k) -> p m k", m=BATCH_TILES)
+            for part, part_k in z_parts:
+                lo = max(first_k, part_k)
+                hi = min(first_k + Z_UNIT_K, part_k + part.shape[1])
+                if lo < hi:
+                    nc.sync.dma_start(
+                        out=by_batch_tile[:, :, lo - first_k : hi - first_k],
+                        in_=part[:, lo - part_k : hi - part_k].rearrange("(m p) k -> p m k", p=P),
+                    )
+
+        def transpose_and_regroup(n):
+            is_z = units[n][0]
+            words = raw_tiles[n][:].bitcast(F32)
+            if is_z:
+                blocks = words.rearrange("p (a b w) -> p a b w", a=2, b=UNIT_BANKS)
+            else:
+                blocks = words.rearrange("p (b a w) -> p a b w", a=2, b=UNIT_BANKS)
+            grouped = grouped_pool.tile([P, UNIT_COLS], BF16, align_bytes=64)
+            grouped_tiles[n] = grouped
+            grouped_words = grouped[:].bitcast(F32).rearrange(
+                "p (b a r u) -> p b a r u", b=UNIT_BANKS, a=2, u=2
+            )
+            for b in range(UNIT_BANKS):
+                bank = ring.tile([P, 2, 2, P], F32)
+                for a in range(2):
+                    for u in range(2):
+                        nc.tensor.transpose(
+                            out=bank[:, a, u, :], in_=blocks[:, a, b, u * P : (u + 1) * P], identity=ident[:]
+                        )
+                joined = bank[:].rearrange("p a u r -> p a r u")
+                if b == VECTOR_BANK:
+                    nc.vector.tensor_copy(out=grouped_words[:, b], in_=joined)
+                else:
+                    nc.scalar.copy(out=grouped_words[:, b], in_=joined)
+
+        def quantise(n):
+            pool = z_mx_pool if units[n][0] else w_mx_pool
+            codes = pool.tile([P, UNIT_CODES], U32, align_bytes=64)
+            scales = pool.tile([P, UNIT_CODES], U8, align_bytes=64)
+            mx_tiles[units[n]] = (codes, scales)
+            nc.vector.quantize_mx(
+                out=codes[:].bitcast(FP8X4), scales=scales[:], in_=grouped_tiles[n][:]
+            )
+
+        def multiply(n):
+            is_z, s, gate = units[n]
+            w_codes, w_scales = mx_tiles[units[n]]
+            for j in range(W_UNIT_PASSES):
+                z_codes, z_scales = mx_tiles[(True, s, j // Z_UNIT_PASSES)]
+                w_cols = slice(j * HIDDEN, (j + 1) * HIDDEN)
+                z_cols = slice((j % Z_UNIT_PASSES) * BATCH, (j % Z_UNIT_PASSES + 1) * BATCH)
+                nc.tensor.matmul_mx(
+                    out=acc[gate][:],
+                    lhsT=w_codes[:, w_cols].bitcast(FP8X4),
+                    lhsT_scale=w_scales[:, w_cols],
+                    rhs=z_codes[:, z_cols].bitcast(FP8X4),
+                    rhs_scale=z_scales[:, z_cols],
+                    start=(s == 0 and j == 0),
+                    stop=(s == SETS - 1 and j == W_UNIT_PASSES - 1),
+                )
+
+        for n in range(RAW_BUFS):
+            load(n)
+
+        old_rows = const.tile([P, BATCH_TILES, HIDDEN], BF16)
+        nc.scalar.dma_start(out=old_rows[:], in_=old_state.rearrange("(m p) h -> p m h", p=P))
+        bias_rows = const.tile([P, HIDDEN], BF16)
+        nc.vector.memset(bias_rows[:], 0.0)
+        for gate in range(GATES):
+            nc.scalar.dma_start(out=bias_rows[gate : gate + 1, :], in_=biases[gate].unsqueeze(0))
+
+        dummy = const.tile([P, 1], F32)
+        nc.vector.memset(dummy[:], 0.0)
+        nc.scalar.activation(out=dummy[:], in_=dummy[:], func=ACT.Sigmoid)
+
+        ident = const.tile([P, P], F32)
+        make_identity(nc, ident[:])
+
+        acc = [acc_pool.tile([P, BATCH], F32, name="acc%d" % gate) for gate in range(GATES)]
+
+        old_rows_f32 = const.tile([P, BATCH_TILES, HIDDEN], F32)
+        nc.vector.tensor_copy(out=old_rows_f32[:], in_=old_rows[:])
+        bias_rows_f32 = const.tile([P, HIDDEN], F32)
+        nc.vector.tensor_copy(out=bias_rows_f32[:], in_=bias_rows[:])
+        bank = ring.tile([P, 2, 2, P], F32)
+        for m in range(BATCH_TILES):
+            nc.tensor.transpose(out=bank[:, 0, m, :], in_=old_rows_f32[:, m, :], identity=ident[:])
+        nc.tensor.transpose(out=bank[:, 1, 0, :], in_=bias_rows_f32[:], identity=ident[:])
+        old_t = const.tile([P, BATCH], F32)
+        nc.vector.tensor_copy(out=old_t[:], in_=bank[:, 0].rearrange("p m b -> p (m b)"))
+        bias_cols = const.tile([P, GATES], F32)
+        nc.vector.tensor_copy(out=bias_cols[:], in_=bank[:, 1, 0, 0:GATES])
+
+        for n in range(n_units + 2):
+            if 1 <= n <= n_units:
+                quantise(n - 1)
+            if n < n_units:
+                transpose_and_regroup(n)
+            if n >= 2 and not units[n - 2][0]:
+                multiply(n - 2)
+            if n + RAW_BUFS < n_units:
+                load(n + RAW_BUFS)
+
+        def gate_value(gate, func, name):
+            value = cell.tile([P, BATCH], F32, name=name)
+            nc.scalar.activation(
+                out=value[:], in_=acc[gate][:], func=func, bias=bias_cols[:, gate : gate + 1], scale=1.0
+            )
+            return value
+
+        input_gate = gate_value(GATE_I, ACT.Sigmoid, "input_gate")
+        forget_gate = gate_value(GATE_F, ACT.Sigmoid, "forget_gate")
+        candidate = gate_value(GATE_S, ACT.Tanh, "candidate")
+        kept = cell.tile([P, BATCH], F32)
+        nc.vector.tensor_tensor(out=kept[:], in0=forget_gate[:], in1=old_t[:], op=ALU.mult)
+        added = cell.tile([P, BATCH], F32)
+        nc.vector.tensor_tensor(out=added[:], in0=input_gate[:], in1=candidate[:], op=ALU.mult)
+        new_state = cell.tile([P, BATCH], F32)
+        nc.vector.tensor_tensor(out=new_state[:], in0=kept[:], in1=added[:], op=ALU.add)
+        state_tanh = cell.tile([P, BATCH], F32)
+        nc.scalar.activation(out=state_tanh[:], in_=new_state[:], func=ACT.Tanh)
+        output_gate = gate_value(GATE_O, ACT.Sigmoid, "output_gate")
+        hidden_t = cell.tile([P, BATCH], F32)
+        nc.vector.tensor_tensor(out=hidden_t[:], in0=output_gate[:], in1=state_tanh[:], op=ALU.mult)
+
+        hidden = cell.tile([P, BATCH_TILES, HIDDEN], F32)
+        for m in range(BATCH_TILES):
+            bank = ring.tile([P, 2, 2, P], F32)
+            nc.tensor.transpose(out=bank[:, 0, 0, :], in_=hidden_t[:, m * P : (m + 1) * P], identity=ident[:])
+            if m == 0:
+                nc.vector.tensor_copy(out=hidden[:, m, :], in_=bank[:, 0, 0, :])
+            else:
+                nc.scalar.copy(out=hidden[:, m, :], in_=bank[:, 0, 0, :])
+        nc.sync.dma_start(out=out.rearrange("(m p) h -> p m h", p=P), in_=hidden[:])

@@ -34,6 +34,7 @@ Z_UNITS_PER_SET = W_UNIT_K // Z_UNIT_K
 
 RAW_BUFS = 8
 VECTOR_BANK = UNIT_BANKS - 1
+PASSES_PER_ROUND = 6
 
 
 def tile_rnn_unit_k_kernel(
@@ -56,13 +57,17 @@ def tile_rnn_unit_k_kernel(
         units.extend([(True, s, half) for half in range(Z_UNITS_PER_SET)])
         units.extend([(False, s, gate) for gate in range(GATES)])
     n_units = len(units)
+    passes = []
+    for n in range(n_units):
+        if not units[n][0]:
+            passes.extend([(n, j) for j in range(W_UNIT_PASSES)])
 
     with ExitStack() as stack:
         const = stack.enter_context(tc.tile_pool(name="const", bufs=1))
         raw_pool = stack.enter_context(tc.tile_pool(name="raw", bufs=RAW_BUFS))
         grouped_pool = stack.enter_context(tc.tile_pool(name="grouped", bufs=3))
         z_mx_pool = stack.enter_context(tc.tile_pool(name="z_mx", bufs=2 * Z_UNITS_PER_SET))
-        w_mx_pool = stack.enter_context(tc.tile_pool(name="w_mx", bufs=3))
+        w_mx_pool = stack.enter_context(tc.tile_pool(name="w_mx", bufs=4))
         cell = stack.enter_context(tc.tile_pool(name="cell", bufs=1))
         acc_pool = stack.enter_context(tc.psum_pool(name="acc", bufs=1))
         ring = stack.enter_context(tc.psum_pool(name="ring", bufs=UNIT_BANKS))
@@ -124,22 +129,21 @@ def tile_rnn_unit_k_kernel(
                 out=codes[:].bitcast(FP8X4), scales=scales[:], in_=grouped_tiles[n][:]
             )
 
-        def multiply(n):
+        def multiply(n, j):
             is_z, s, gate = units[n]
             w_codes, w_scales = mx_tiles[units[n]]
-            for j in range(W_UNIT_PASSES):
-                z_codes, z_scales = mx_tiles[(True, s, j // Z_UNIT_PASSES)]
-                w_cols = slice(j * HIDDEN, (j + 1) * HIDDEN)
-                z_cols = slice((j % Z_UNIT_PASSES) * BATCH, (j % Z_UNIT_PASSES + 1) * BATCH)
-                nc.tensor.matmul_mx(
-                    out=acc[gate][:],
-                    lhsT=w_codes[:, w_cols].bitcast(FP8X4),
-                    lhsT_scale=w_scales[:, w_cols],
-                    rhs=z_codes[:, z_cols].bitcast(FP8X4),
-                    rhs_scale=z_scales[:, z_cols],
-                    start=(s == 0 and j == 0),
-                    stop=(s == SETS - 1 and j == W_UNIT_PASSES - 1),
-                )
+            z_codes, z_scales = mx_tiles[(True, s, j // Z_UNIT_PASSES)]
+            w_cols = slice(j * HIDDEN, (j + 1) * HIDDEN)
+            z_cols = slice((j % Z_UNIT_PASSES) * BATCH, (j % Z_UNIT_PASSES + 1) * BATCH)
+            nc.tensor.matmul_mx(
+                out=acc[gate][:],
+                lhsT=w_codes[:, w_cols].bitcast(FP8X4),
+                lhsT_scale=w_scales[:, w_cols],
+                rhs=z_codes[:, z_cols].bitcast(FP8X4),
+                rhs_scale=z_scales[:, z_cols],
+                start=(s == 0 and j == 0),
+                stop=(s == SETS - 1 and j == W_UNIT_PASSES - 1),
+            )
 
         for n in range(RAW_BUFS):
             load(n)
@@ -173,13 +177,17 @@ def tile_rnn_unit_k_kernel(
         bias_cols = const.tile([P, GATES], F32)
         nc.vector.tensor_copy(out=bias_cols[:], in_=bank[:, 1, 0, 0:GATES])
 
+        issued = 0
         for n in range(n_units + 2):
             if 1 <= n <= n_units:
                 quantise(n - 1)
             if n < n_units:
                 transpose_and_regroup(n)
-            if n >= 2 and not units[n - 2][0]:
-                multiply(n - 2)
+            ready = len([p for p in passes if p[0] <= n - 2])
+            upto = min(ready, issued + PASSES_PER_ROUND) if n < n_units else ready
+            for unit, j in passes[issued:upto]:
+                multiply(unit, j)
+            issued = upto
             if n + RAW_BUFS < n_units:
                 load(n + RAW_BUFS)
 

@@ -17,24 +17,26 @@ BATCH_TILES = BATCH // P
 HIDDEN = 128
 K = 16384
 K_PASS = 512
+PASS_WORDS = K_PASS // 2
 GATES = 4
+Z = "z"
 
 FLOPS = 2 * BATCH * GATES * HIDDEN * K
 
-UNIT_COLS = 4096
-UNIT_WORDS = UNIT_COLS // 2
-UNIT_CODES = UNIT_COLS // 4
+BANK_PIECES = 2
+BANK_CODES = BANK_PIECES * P
 UNIT_BANKS = 4
-W_UNIT_K = UNIT_COLS
-Z_UNIT_K = UNIT_COLS // BATCH_TILES
-W_UNIT_PASSES = W_UNIT_K // K_PASS
-Z_UNIT_PASSES = Z_UNIT_K // K_PASS
-SETS = K // W_UNIT_K
-Z_UNITS_PER_SET = W_UNIT_K // Z_UNIT_K
-
-RAW_BUFS = 8
+UNIT_COLS = UNIT_BANKS * BANK_PIECES * K_PASS
+UNIT_CODES = UNIT_BANKS * BANK_CODES
 VECTOR_BANK = UNIT_BANKS - 1
-PASSES_PER_ROUND = 6
+
+FIRST_SET_K = 1024
+WIDEST_SET_K = UNIT_COLS
+Z_LOAD_K = UNIT_COLS // BATCH_TILES
+
+RAW_BUFS = 10
+MX_BUFS = 10
+PASSES_PER_UNIT = 5
 
 
 def tile_rnn_unit_k_kernel(
@@ -52,22 +54,45 @@ def tile_rnn_unit_k_kernel(
         (previous_layer, input_x.shape[1] + previous_time.shape[1]),
     ]
 
-    units = []
-    for s in range(SETS):
-        units.extend([(True, s, half) for half in range(Z_UNITS_PER_SET)])
-        units.extend([(False, s, gate) for gate in range(GATES)])
-    n_units = len(units)
+    loads = []
+    set_k = 0
+    while set_k < K:
+        width = min(max(set_k, FIRST_SET_K), WIDEST_SET_K)
+        z_width = min(width, Z_LOAD_K)
+        loads.extend([(Z, k, z_width) for k in range(set_k, set_k + width, z_width)])
+        loads.extend([(gate, set_k, width) for gate in range(GATES)])
+        set_k += width
+    n_loads = len(loads)
+
+    banks = []
+    for i in range(n_loads):
+        who, first_k, width = loads[i]
+        k_per_bank = K_PASS if who == Z else BANK_PIECES * K_PASS
+        banks.extend([(i, c) for c in range(width // k_per_bank)])
+    n_units = len(banks) // UNIT_BANKS
+    last_unit_of_load = {}
+
+    place = {}
     passes = []
-    for n in range(n_units):
-        if not units[n][0]:
-            passes.extend([(n, j) for j in range(W_UNIT_PASSES)])
+    for position in range(len(banks)):
+        i, c = banks[position]
+        who, first_k, width = loads[i]
+        unit = position // UNIT_BANKS
+        column = (position % UNIT_BANKS) * BANK_CODES
+        last_unit_of_load[i] = unit
+        if who == Z:
+            place[(Z, first_k // K_PASS + c)] = (unit, column)
+        else:
+            for a in range(BANK_PIECES):
+                g = first_k // K_PASS + BANK_PIECES * c + a
+                place[(who, g)] = (unit, column + a * P)
+                passes.append((who, g))
 
     with ExitStack() as stack:
         const = stack.enter_context(tc.tile_pool(name="const", bufs=1))
         raw_pool = stack.enter_context(tc.tile_pool(name="raw", bufs=RAW_BUFS))
         grouped_pool = stack.enter_context(tc.tile_pool(name="grouped", bufs=3))
-        z_mx_pool = stack.enter_context(tc.tile_pool(name="z_mx", bufs=2 * Z_UNITS_PER_SET))
-        w_mx_pool = stack.enter_context(tc.tile_pool(name="w_mx", bufs=4))
+        mx_pool = stack.enter_context(tc.tile_pool(name="mx", bufs=MX_BUFS))
         cell = stack.enter_context(tc.tile_pool(name="cell", bufs=1))
         acc_pool = stack.enter_context(tc.psum_pool(name="acc", bufs=1))
         ring = stack.enter_context(tc.psum_pool(name="ring", bufs=UNIT_BANKS))
@@ -77,42 +102,46 @@ def tile_rnn_unit_k_kernel(
         grouped_tiles = {}
         mx_tiles = {}
 
-        def load(n):
-            is_z, s, index = units[n]
+        def load(i):
+            who, first_k, width = loads[i]
             raw = raw_pool.tile([P, UNIT_COLS], BF16)
-            raw_tiles[n] = raw
-            if not is_z:
-                nc.sync.dma_start(out=raw[:], in_=weights[index][:, s * W_UNIT_K : (s + 1) * W_UNIT_K])
+            raw_tiles[i] = raw
+            if who != Z:
+                nc.sync.dma_start(out=raw[:, 0:width], in_=weights[who][:, first_k : first_k + width])
                 return
-            first_k = s * W_UNIT_K + index * Z_UNIT_K
-            by_batch_tile = raw[:].rearrange("p (m k) -> p m k", m=BATCH_TILES)
+            by_batch_tile = raw[:, 0 : BATCH_TILES * width].rearrange("p (m k) -> p m k", m=BATCH_TILES)
             for part, part_k in z_parts:
                 lo = max(first_k, part_k)
-                hi = min(first_k + Z_UNIT_K, part_k + part.shape[1])
+                hi = min(first_k + width, part_k + part.shape[1])
                 if lo < hi:
                     nc.sync.dma_start(
                         out=by_batch_tile[:, :, lo - first_k : hi - first_k],
                         in_=part[:, lo - part_k : hi - part_k].rearrange("(m p) k -> p m k", p=P),
                     )
 
+        def bank_pieces(i, c):
+            who, first_k, width = loads[i]
+            if who == Z:
+                words = raw_tiles[i][:, 0 : BATCH_TILES * width].bitcast(F32)
+                by_batch_tile = words.rearrange("p (m w) -> p m w", m=BATCH_TILES)
+                return by_batch_tile[:, :, c * PASS_WORDS : (c + 1) * PASS_WORDS]
+            words = raw_tiles[i][:, 0:width].bitcast(F32)
+            return words.rearrange("p (c a w) -> p c a w", a=BANK_PIECES, w=PASS_WORDS)[:, c]
+
         def transpose_and_regroup(n):
-            is_z = units[n][0]
-            words = raw_tiles[n][:].bitcast(F32)
-            if is_z:
-                blocks = words.rearrange("p (a b w) -> p a b w", a=2, b=UNIT_BANKS)
-            else:
-                blocks = words.rearrange("p (b a w) -> p a b w", a=2, b=UNIT_BANKS)
             grouped = grouped_pool.tile([P, UNIT_COLS], BF16, align_bytes=64)
             grouped_tiles[n] = grouped
             grouped_words = grouped[:].bitcast(F32).rearrange(
-                "p (b a r u) -> p b a r u", b=UNIT_BANKS, a=2, u=2
+                "p (b a r u) -> p b a r u", b=UNIT_BANKS, a=BANK_PIECES, u=2
             )
             for b in range(UNIT_BANKS):
-                bank = ring.tile([P, 2, 2, P], F32)
-                for a in range(2):
+                i, c = banks[n * UNIT_BANKS + b]
+                pieces = bank_pieces(i, c)
+                bank = ring.tile([P, BANK_PIECES, 2, P], F32)
+                for a in range(BANK_PIECES):
                     for u in range(2):
                         nc.tensor.transpose(
-                            out=bank[:, a, u, :], in_=blocks[:, a, b, u * P : (u + 1) * P], identity=ident[:]
+                            out=bank[:, a, u, :], in_=pieces[:, a, u * P : (u + 1) * P], identity=ident[:]
                         )
                 joined = bank[:].rearrange("p a u r -> p a r u")
                 if b == VECTOR_BANK:
@@ -121,32 +150,27 @@ def tile_rnn_unit_k_kernel(
                     nc.scalar.copy(out=grouped_words[:, b], in_=joined)
 
         def quantise(n):
-            pool = z_mx_pool if units[n][0] else w_mx_pool
-            codes = pool.tile([P, UNIT_CODES], U32, align_bytes=64)
-            scales = pool.tile([P, UNIT_CODES], U8, align_bytes=64)
-            mx_tiles[units[n]] = (codes, scales)
-            nc.vector.quantize_mx(
-                out=codes[:].bitcast(FP8X4), scales=scales[:], in_=grouped_tiles[n][:]
-            )
+            codes = mx_pool.tile([P, UNIT_CODES], U32, align_bytes=64)
+            scales = mx_pool.tile([P, UNIT_CODES], U8, align_bytes=64)
+            mx_tiles[n] = (codes, scales)
+            nc.vector.quantize_mx(out=codes[:].bitcast(FP8X4), scales=scales[:], in_=grouped_tiles[n][:])
 
-        def multiply(n, j):
-            is_z, s, gate = units[n]
-            w_codes, w_scales = mx_tiles[units[n]]
-            z_codes, z_scales = mx_tiles[(True, s, j // Z_UNIT_PASSES)]
-            w_cols = slice(j * HIDDEN, (j + 1) * HIDDEN)
-            z_cols = slice((j % Z_UNIT_PASSES) * BATCH, (j % Z_UNIT_PASSES + 1) * BATCH)
+        def multiply(gate, g):
+            w_unit, w_column = place[(gate, g)]
+            z_unit, z_column = place[(Z, g)]
+            w_codes, w_scales = mx_tiles[w_unit]
+            z_codes, z_scales = mx_tiles[z_unit]
+            w_cols = slice(w_column, w_column + HIDDEN)
+            z_cols = slice(z_column, z_column + BATCH)
             nc.tensor.matmul_mx(
                 out=acc[gate][:],
                 lhsT=w_codes[:, w_cols].bitcast(FP8X4),
                 lhsT_scale=w_scales[:, w_cols],
                 rhs=z_codes[:, z_cols].bitcast(FP8X4),
                 rhs_scale=z_scales[:, z_cols],
-                start=(s == 0 and j == 0),
-                stop=(s == SETS - 1 and j == W_UNIT_PASSES - 1),
+                start=(g == 0),
+                stop=(g == K // K_PASS - 1),
             )
-
-        for n in range(RAW_BUFS):
-            load(n)
 
         old_rows = const.tile([P, BATCH_TILES, HIDDEN], BF16)
         nc.scalar.dma_start(out=old_rows[:], in_=old_state.rearrange("(m p) h -> p m h", p=P))
@@ -154,6 +178,8 @@ def tile_rnn_unit_k_kernel(
         nc.vector.memset(bias_rows[:], 0.0)
         for gate in range(GATES):
             nc.scalar.dma_start(out=bias_rows[gate : gate + 1, :], in_=biases[gate].unsqueeze(0))
+        for i in range(RAW_BUFS):
+            load(i)
 
         dummy = const.tile([P, 1], F32)
         nc.vector.memset(dummy[:], 0.0)
@@ -164,32 +190,37 @@ def tile_rnn_unit_k_kernel(
 
         acc = [acc_pool.tile([P, BATCH], F32, name="acc%d" % gate) for gate in range(GATES)]
 
-        old_rows_f32 = const.tile([P, BATCH_TILES, HIDDEN], F32)
-        nc.vector.tensor_copy(out=old_rows_f32[:], in_=old_rows[:])
-        bias_rows_f32 = const.tile([P, HIDDEN], F32)
-        nc.vector.tensor_copy(out=bias_rows_f32[:], in_=bias_rows[:])
-        bank = ring.tile([P, 2, 2, P], F32)
-        for m in range(BATCH_TILES):
-            nc.tensor.transpose(out=bank[:, 0, m, :], in_=old_rows_f32[:, m, :], identity=ident[:])
-        nc.tensor.transpose(out=bank[:, 1, 0, :], in_=bias_rows_f32[:], identity=ident[:])
         old_t = const.tile([P, BATCH], F32)
-        nc.vector.tensor_copy(out=old_t[:], in_=bank[:, 0].rearrange("p m b -> p (m b)"))
         bias_cols = const.tile([P, GATES], F32)
-        nc.vector.tensor_copy(out=bias_cols[:], in_=bank[:, 1, 0, 0:GATES])
+
+        def prepare_cell_operands():
+            old_rows_f32 = const.tile([P, BATCH_TILES, HIDDEN], F32)
+            nc.vector.tensor_copy(out=old_rows_f32[:], in_=old_rows[:])
+            bias_rows_f32 = const.tile([P, HIDDEN], F32)
+            nc.vector.tensor_copy(out=bias_rows_f32[:], in_=bias_rows[:])
+            bank = ring.tile([P, BANK_PIECES, 2, P], F32)
+            for m in range(BATCH_TILES):
+                nc.tensor.transpose(out=bank[:, 0, m, :], in_=old_rows_f32[:, m, :], identity=ident[:])
+            nc.tensor.transpose(out=bank[:, 1, 0, :], in_=bias_rows_f32[:], identity=ident[:])
+            nc.vector.tensor_copy(out=old_t[:], in_=bank[:, 0].rearrange("p m b -> p (m b)"))
+            nc.vector.tensor_copy(out=bias_cols[:], in_=bank[:, 1, 0, 0:GATES])
 
         issued = 0
-        for n in range(n_units + 2):
-            if 1 <= n <= n_units:
+        for n in range(n_units + 1):
+            if n >= 1:
                 quantise(n - 1)
             if n < n_units:
                 transpose_and_regroup(n)
-            ready = len([p for p in passes if p[0] <= n - 2])
-            upto = min(ready, issued + PASSES_PER_ROUND) if n < n_units else ready
-            for unit, j in passes[issued:upto]:
-                multiply(unit, j)
+            if n == 0:
+                prepare_cell_operands()
+            ready = len([p for p in passes if place[p][0] <= n - 1])
+            upto = min(ready, issued + PASSES_PER_UNIT) if n < n_units else ready
+            for gate, g in passes[issued:upto]:
+                multiply(gate, g)
             issued = upto
-            if n + RAW_BUFS < n_units:
-                load(n + RAW_BUFS)
+            for i in range(RAW_BUFS, n_loads):
+                if last_unit_of_load[i - RAW_BUFS] == n:
+                    load(i)
 
         def gate_value(gate, func, name):
             value = cell.tile([P, BATCH], F32, name=name)
@@ -215,7 +246,7 @@ def tile_rnn_unit_k_kernel(
 
         hidden = cell.tile([P, BATCH_TILES, HIDDEN], F32)
         for m in range(BATCH_TILES):
-            bank = ring.tile([P, 2, 2, P], F32)
+            bank = ring.tile([P, BANK_PIECES, 2, P], F32)
             nc.tensor.transpose(out=bank[:, 0, 0, :], in_=hidden_t[:, m * P : (m + 1) * P], identity=ident[:])
             if m == 0:
                 nc.vector.tensor_copy(out=hidden[:, m, :], in_=bank[:, 0, 0, :])

@@ -34,9 +34,11 @@ FIRST_SET_K = 1024
 WIDEST_SET_K = UNIT_COLS
 Z_LOAD_K = UNIT_COLS // BATCH_TILES
 
+LAST_LOAD_K = 1024
+
 RAW_BUFS = 10
 MX_BUFS = 10
-PASSES_PER_UNIT = 5
+PASSES_PER_UNIT = 6
 
 
 def tile_rnn_unit_k_kernel(
@@ -62,6 +64,14 @@ def tile_rnn_unit_k_kernel(
         loads.extend([(Z, k, z_width) for k in range(set_k, set_k + width, z_width)])
         loads.extend([(gate, set_k, width) for gate in range(GATES)])
         set_k += width
+    who, first_k, width = loads[-1]
+    loads = loads[:-1]
+    n_whole_loads = len(loads)
+    while width > LAST_LOAD_K:
+        width = width // 2
+        loads.append((who, first_k, width))
+        first_k += width
+    loads.append((who, first_k, width))
     n_loads = len(loads)
 
     banks = []
@@ -69,24 +79,31 @@ def tile_rnn_unit_k_kernel(
         who, first_k, width = loads[i]
         k_per_bank = K_PASS if who == Z else BANK_PIECES * K_PASS
         banks.extend([(i, c) for c in range(width // k_per_bank)])
-    n_units = len(banks) // UNIT_BANKS
+
+    n_whole_banks = len([bank for bank in banks if bank[0] < n_whole_loads])
+    units = [(position, UNIT_BANKS) for position in range(0, n_whole_banks, UNIT_BANKS)]
+    for i in range(n_whole_loads, n_loads):
+        positions = [position for position in range(len(banks)) if banks[position][0] == i]
+        units.append((positions[0], len(positions)))
+    n_units = len(units)
     last_unit_of_load = {}
 
     place = {}
     passes = []
-    for position in range(len(banks)):
-        i, c = banks[position]
-        who, first_k, width = loads[i]
-        unit = position // UNIT_BANKS
-        column = (position % UNIT_BANKS) * BANK_CODES
-        last_unit_of_load[i] = unit
-        if who == Z:
-            place[(Z, first_k // K_PASS + c)] = (unit, column)
-        else:
-            for a in range(BANK_PIECES):
-                g = first_k // K_PASS + BANK_PIECES * c + a
-                place[(who, g)] = (unit, column + a * P)
-                passes.append((who, g))
+    for unit in range(n_units):
+        first_bank, n_banks = units[unit]
+        for b in range(n_banks):
+            i, c = banks[first_bank + b]
+            who, first_k, width = loads[i]
+            column = b * BANK_CODES
+            last_unit_of_load[i] = unit
+            if who == Z:
+                place[(Z, first_k // K_PASS + c)] = (unit, column)
+            else:
+                for a in range(BANK_PIECES):
+                    g = first_k // K_PASS + BANK_PIECES * c + a
+                    place[(who, g)] = (unit, column + a * P)
+                    passes.append((who, g))
 
     with ExitStack() as stack:
         const = stack.enter_context(tc.tile_pool(name="const", bufs=1))
@@ -129,13 +146,14 @@ def tile_rnn_unit_k_kernel(
             return words.rearrange("p (c a w) -> p c a w", a=BANK_PIECES, w=PASS_WORDS)[:, c]
 
         def transpose_and_regroup(n):
+            first_bank, n_banks = units[n]
             grouped = grouped_pool.tile([P, UNIT_COLS], BF16, align_bytes=64)
             grouped_tiles[n] = grouped
             grouped_words = grouped[:].bitcast(F32).rearrange(
                 "p (b a r u) -> p b a r u", b=UNIT_BANKS, a=BANK_PIECES, u=2
             )
-            for b in range(UNIT_BANKS):
-                i, c = banks[n * UNIT_BANKS + b]
+            for b in range(n_banks):
+                i, c = banks[first_bank + b]
                 pieces = bank_pieces(i, c)
                 bank = ring.tile([P, BANK_PIECES, 2, P], F32)
                 for a in range(BANK_PIECES):
@@ -153,7 +171,12 @@ def tile_rnn_unit_k_kernel(
             codes = mx_pool.tile([P, UNIT_CODES], U32, align_bytes=64)
             scales = mx_pool.tile([P, UNIT_CODES], U8, align_bytes=64)
             mx_tiles[n] = (codes, scales)
-            nc.vector.quantize_mx(out=codes[:].bitcast(FP8X4), scales=scales[:], in_=grouped_tiles[n][:])
+            n_codes = units[n][1] * BANK_CODES
+            nc.vector.quantize_mx(
+                out=codes[:, 0:n_codes].bitcast(FP8X4),
+                scales=scales[:, 0:n_codes],
+                in_=grouped_tiles[n][:, 0 : 4 * n_codes],
+            )
 
         def multiply(gate, g):
             w_unit, w_column = place[(gate, g)]

@@ -17,28 +17,26 @@ BATCH_TILES = BATCH // P
 HIDDEN = 128
 K = 16384
 K_PASS = 512
-PASS_WORDS = K_PASS // 2
 GATES = 4
 Z = "z"
 
 FLOPS = 2 * BATCH * GATES * HIDDEN * K
 
-BANK_PIECES = 2
-BANK_CODES = BANK_PIECES * P
+UNIT_COLS = 4096
+UNIT_CODES = UNIT_COLS // 4
 UNIT_BANKS = 4
-UNIT_COLS = UNIT_BANKS * BANK_PIECES * K_PASS
-UNIT_CODES = UNIT_BANKS * BANK_CODES
+BANK_PIECES = 2
+W_UNIT_K = UNIT_COLS
+Z_UNIT_K = UNIT_COLS // BATCH_TILES
+W_UNIT_PASSES = W_UNIT_K // K_PASS
+Z_UNIT_PASSES = Z_UNIT_K // K_PASS
+SETS = K // W_UNIT_K
+Z_UNITS_PER_SET = W_UNIT_K // Z_UNIT_K
 VECTOR_BANK = UNIT_BANKS - 1
 
-FIRST_SET_K = 1024
-WIDEST_SET_K = UNIT_COLS
-Z_LOAD_K = UNIT_COLS // BATCH_TILES
-
-LAST_LOAD_K = 1024
-
 RAW_BUFS = 10
-MX_BUFS = 10
-PASSES_PER_UNIT = 6
+MX_BUFS = 13
+PASSES_PER_UNIT = 5
 
 
 def tile_rnn_unit_k_kernel(
@@ -56,54 +54,17 @@ def tile_rnn_unit_k_kernel(
         (previous_layer, input_x.shape[1] + previous_time.shape[1]),
     ]
 
-    loads = []
-    set_k = 0
-    while set_k < K:
-        width = min(max(set_k, FIRST_SET_K), WIDEST_SET_K)
-        z_width = min(width, Z_LOAD_K)
-        loads.extend([(Z, k, z_width) for k in range(set_k, set_k + width, z_width)])
-        loads.extend([(gate, set_k, width) for gate in range(GATES)])
-        set_k += width
-    who, first_k, width = loads[-1]
-    loads = loads[:-1]
-    n_whole_loads = len(loads)
-    while width > LAST_LOAD_K:
-        width = width // 2
-        loads.append((who, first_k, width))
-        first_k += width
-    loads.append((who, first_k, width))
-    n_loads = len(loads)
-
-    banks = []
-    for i in range(n_loads):
-        who, first_k, width = loads[i]
-        k_per_bank = K_PASS if who == Z else BANK_PIECES * K_PASS
-        banks.extend([(i, c) for c in range(width // k_per_bank)])
-
-    n_whole_banks = len([bank for bank in banks if bank[0] < n_whole_loads])
-    units = [(position, UNIT_BANKS) for position in range(0, n_whole_banks, UNIT_BANKS)]
-    for i in range(n_whole_loads, n_loads):
-        positions = [position for position in range(len(banks)) if banks[position][0] == i]
-        units.append((positions[0], len(positions)))
+    units = [(Z, half) for half in range(Z_UNITS_PER_SET)]
+    for s in range(SETS):
+        for half in range(Z_UNITS_PER_SET):
+            units.extend([(gate, s) for gate in range(2 * half, 2 * half + 2)])
+            if s + 1 < SETS:
+                units.append((Z, Z_UNITS_PER_SET * (s + 1) + half))
     n_units = len(units)
-    last_unit_of_load = {}
-
-    place = {}
     passes = []
-    for unit in range(n_units):
-        first_bank, n_banks = units[unit]
-        for b in range(n_banks):
-            i, c = banks[first_bank + b]
-            who, first_k, width = loads[i]
-            column = b * BANK_CODES
-            last_unit_of_load[i] = unit
-            if who == Z:
-                place[(Z, first_k // K_PASS + c)] = (unit, column)
-            else:
-                for a in range(BANK_PIECES):
-                    g = first_k // K_PASS + BANK_PIECES * c + a
-                    place[(who, g)] = (unit, column + a * P)
-                    passes.append((who, g))
+    for n in range(n_units):
+        if units[n][0] != Z:
+            passes.extend([(n, j) for j in range(W_UNIT_PASSES)])
 
     with ExitStack() as stack:
         const = stack.enter_context(tc.tile_pool(name="const", bufs=1))
@@ -119,47 +80,41 @@ def tile_rnn_unit_k_kernel(
         grouped_tiles = {}
         mx_tiles = {}
 
-        def load(i):
-            who, first_k, width = loads[i]
+        def load(n):
+            who, index = units[n]
             raw = raw_pool.tile([P, UNIT_COLS], BF16)
-            raw_tiles[i] = raw
+            raw_tiles[n] = raw
             if who != Z:
-                nc.sync.dma_start(out=raw[:, 0:width], in_=weights[who][:, first_k : first_k + width])
+                nc.sync.dma_start(out=raw[:], in_=weights[who][:, index * W_UNIT_K : (index + 1) * W_UNIT_K])
                 return
-            by_batch_tile = raw[:, 0 : BATCH_TILES * width].rearrange("p (m k) -> p m k", m=BATCH_TILES)
+            first_k = index * Z_UNIT_K
+            by_batch_tile = raw[:].rearrange("p (m k) -> p m k", m=BATCH_TILES)
             for part, part_k in z_parts:
                 lo = max(first_k, part_k)
-                hi = min(first_k + width, part_k + part.shape[1])
+                hi = min(first_k + Z_UNIT_K, part_k + part.shape[1])
                 if lo < hi:
                     nc.sync.dma_start(
                         out=by_batch_tile[:, :, lo - first_k : hi - first_k],
                         in_=part[:, lo - part_k : hi - part_k].rearrange("(m p) k -> p m k", p=P),
                     )
 
-        def bank_pieces(i, c):
-            who, first_k, width = loads[i]
-            if who == Z:
-                words = raw_tiles[i][:, 0 : BATCH_TILES * width].bitcast(F32)
-                by_batch_tile = words.rearrange("p (m w) -> p m w", m=BATCH_TILES)
-                return by_batch_tile[:, :, c * PASS_WORDS : (c + 1) * PASS_WORDS]
-            words = raw_tiles[i][:, 0:width].bitcast(F32)
-            return words.rearrange("p (c a w) -> p c a w", a=BANK_PIECES, w=PASS_WORDS)[:, c]
-
         def transpose_and_regroup(n):
-            first_bank, n_banks = units[n]
+            words = raw_tiles[n][:].bitcast(F32)
+            if units[n][0] == Z:
+                pieces = words.rearrange("p (a b w) -> p b a w", a=BANK_PIECES, b=UNIT_BANKS)
+            else:
+                pieces = words.rearrange("p (b a w) -> p b a w", a=BANK_PIECES, b=UNIT_BANKS)
             grouped = grouped_pool.tile([P, UNIT_COLS], BF16, align_bytes=64)
             grouped_tiles[n] = grouped
             grouped_words = grouped[:].bitcast(F32).rearrange(
                 "p (b a r u) -> p b a r u", b=UNIT_BANKS, a=BANK_PIECES, u=2
             )
-            for b in range(n_banks):
-                i, c = banks[first_bank + b]
-                pieces = bank_pieces(i, c)
+            for b in range(UNIT_BANKS):
                 bank = ring.tile([P, BANK_PIECES, 2, P], F32)
                 for a in range(BANK_PIECES):
                     for u in range(2):
                         nc.tensor.transpose(
-                            out=bank[:, a, u, :], in_=pieces[:, a, u * P : (u + 1) * P], identity=ident[:]
+                            out=bank[:, a, u, :], in_=pieces[:, b, a, u * P : (u + 1) * P], identity=ident[:]
                         )
                 joined = bank[:].rearrange("p a u r -> p a r u")
                 if b == VECTOR_BANK:
@@ -170,29 +125,23 @@ def tile_rnn_unit_k_kernel(
         def quantise(n):
             codes = mx_pool.tile([P, UNIT_CODES], U32, align_bytes=64)
             scales = mx_pool.tile([P, UNIT_CODES], U8, align_bytes=64)
-            mx_tiles[n] = (codes, scales)
-            n_codes = units[n][1] * BANK_CODES
-            nc.vector.quantize_mx(
-                out=codes[:, 0:n_codes].bitcast(FP8X4),
-                scales=scales[:, 0:n_codes],
-                in_=grouped_tiles[n][:, 0 : 4 * n_codes],
-            )
+            mx_tiles[units[n]] = (codes, scales)
+            nc.vector.quantize_mx(out=codes[:].bitcast(FP8X4), scales=scales[:], in_=grouped_tiles[n][:])
 
-        def multiply(gate, g):
-            w_unit, w_column = place[(gate, g)]
-            z_unit, z_column = place[(Z, g)]
-            w_codes, w_scales = mx_tiles[w_unit]
-            z_codes, z_scales = mx_tiles[z_unit]
-            w_cols = slice(w_column, w_column + HIDDEN)
-            z_cols = slice(z_column, z_column + BATCH)
+        def multiply(n, j):
+            gate, s = units[n]
+            w_codes, w_scales = mx_tiles[units[n]]
+            z_codes, z_scales = mx_tiles[(Z, Z_UNITS_PER_SET * s + j // Z_UNIT_PASSES)]
+            w_cols = slice(j * HIDDEN, (j + 1) * HIDDEN)
+            z_cols = slice((j % Z_UNIT_PASSES) * BATCH, (j % Z_UNIT_PASSES + 1) * BATCH)
             nc.tensor.matmul_mx(
                 out=acc[gate][:],
                 lhsT=w_codes[:, w_cols].bitcast(FP8X4),
                 lhsT_scale=w_scales[:, w_cols],
                 rhs=z_codes[:, z_cols].bitcast(FP8X4),
                 rhs_scale=z_scales[:, z_cols],
-                start=(g == 0),
-                stop=(g == K // K_PASS - 1),
+                start=(s == 0 and j == 0),
+                stop=(s == SETS - 1 and j == W_UNIT_PASSES - 1),
             )
 
         old_rows = const.tile([P, BATCH_TILES, HIDDEN], BF16)
@@ -201,8 +150,8 @@ def tile_rnn_unit_k_kernel(
         nc.vector.memset(bias_rows[:], 0.0)
         for gate in range(GATES):
             nc.scalar.dma_start(out=bias_rows[gate : gate + 1, :], in_=biases[gate].unsqueeze(0))
-        for i in range(RAW_BUFS):
-            load(i)
+        for n in range(RAW_BUFS):
+            load(n)
 
         dummy = const.tile([P, 1], F32)
         nc.vector.memset(dummy[:], 0.0)
@@ -236,14 +185,13 @@ def tile_rnn_unit_k_kernel(
                 transpose_and_regroup(n)
             if n == 0:
                 prepare_cell_operands()
-            ready = len([p for p in passes if place[p][0] <= n - 1])
+            ready = len([p for p in passes if p[0] <= n - 1])
             upto = min(ready, issued + PASSES_PER_UNIT) if n < n_units else ready
-            for gate, g in passes[issued:upto]:
-                multiply(gate, g)
+            for unit, j in passes[issued:upto]:
+                multiply(unit, j)
             issued = upto
-            for i in range(RAW_BUFS, n_loads):
-                if last_unit_of_load[i - RAW_BUFS] == n:
-                    load(i)
+            if n + RAW_BUFS < n_units:
+                load(n + RAW_BUFS)
 
         def gate_value(gate, func, name):
             value = cell.tile([P, BATCH], F32, name=name)

@@ -36,7 +36,7 @@ VECTOR_BANK = UNIT_BANKS - 1
 
 RAW_BUFS = 10
 MX_BUFS = 13
-PASSES_PER_UNIT = 5
+PASSES_PER_UNIT = 6
 
 
 def tile_rnn_unit_k_kernel(
@@ -185,8 +185,8 @@ def tile_rnn_unit_k_kernel(
                 transpose_and_regroup(n)
             if n == 0:
                 prepare_cell_operands()
-            ready = len([p for p in passes if p[0] <= n - 1])
-            upto = min(ready, issued + PASSES_PER_UNIT) if n < n_units else ready
+            ready = len([p for p in passes if p[0] <= n - 2])
+            upto = min(ready, issued + PASSES_PER_UNIT) if n < n_units else len(passes)
             for unit, j in passes[issued:upto]:
                 multiply(unit, j)
             issued = upto

@@ -17,26 +17,26 @@ BATCH_TILES = BATCH // P
 HIDDEN = 128
 K = 16384
 K_PASS = 512
+N_PASSES = K // K_PASS
 GATES = 4
 Z = "z"
 
 FLOPS = 2 * BATCH * GATES * HIDDEN * K
 
-UNIT_COLS = 4096
-UNIT_CODES = UNIT_COLS // 4
-UNIT_BANKS = 4
+PIECE_COLS = K_PASS
+PIECE_WORDS = PIECE_COLS // 2
 BANK_PIECES = 2
-W_UNIT_K = UNIT_COLS
-Z_UNIT_K = UNIT_COLS // BATCH_TILES
-W_UNIT_PASSES = W_UNIT_K // K_PASS
-Z_UNIT_PASSES = Z_UNIT_K // K_PASS
-SETS = K // W_UNIT_K
-Z_UNITS_PER_SET = W_UNIT_K // Z_UNIT_K
-VECTOR_BANK = UNIT_BANKS - 1
+MAX_PIECES = 8
+RING_BANKS = 4
+VECTOR_EVERY = 4
 
 RAW_BUFS = 10
+GROUPED_BUFS = 3
 MX_BUFS = 13
-PASSES_PER_UNIT = 6
+BURST_BANKS = 4
+BURST_PASSES = 6
+LAG_BANKS = 4
+QUANT_PIECES = 4
 
 
 def tile_rnn_unit_k_kernel(
@@ -54,94 +54,201 @@ def tile_rnn_unit_k_kernel(
         (previous_layer, input_x.shape[1] + previous_time.shape[1]),
     ]
 
-    units = [(Z, half) for half in range(Z_UNITS_PER_SET)]
-    for s in range(SETS):
-        for half in range(Z_UNITS_PER_SET):
-            units.extend([(gate, s) for gate in range(2 * half, 2 * half + 2)])
-            if s + 1 < SETS:
-                units.append((Z, Z_UNITS_PER_SET * (s + 1) + half))
+    loads = []
+    units = []
+
+    def z_pieces(g0, n):
+        return [((Z, m), g0 + j) for j in range(n) for m in range(BATCH_TILES)]
+
+    def w_pieces(gates, g0, n):
+        return [(gate, g0 + j) for gate in gates for j in range(n)]
+
+    SET = 8
+    HALF = SET // 2
+    N_SETS = N_PASSES // SET
+
+    def add(spec, pieces):
+        loads.append(spec)
+        units.append(pieces)
+
+    def add_z(s, h):
+        add(("zk", s * SET + h * HALF, HALF), z_pieces(s * SET + h * HALF, HALF))
+
+    add_z(0, 0)
+    add_z(0, 1)
+    for s in range(N_SETS):
+        for h in range(2):
+            for gate in (2 * h, 2 * h + 1):
+                add(("w", (gate,), s * SET, SET), w_pieces((gate,), s * SET, SET))
+            if s + 1 < N_SETS:
+                add_z(s + 1, h)
     n_units = len(units)
+
+    source = {}
+    load_pieces = []
+    for i in range(len(loads)):
+        spec = loads[i]
+        if spec[0] == "zk":
+            kind, g0, n = spec
+            held = [((Z, m), g0 + j) for m in range(BATCH_TILES) for j in range(n)]
+        elif spec[0] == "zm":
+            kind, m, g0, n = spec
+            held = [((Z, m), g0 + j) for j in range(n)]
+        else:
+            kind, gates, g0, n = spec
+            held = [(gate, g0 + j) for gate in gates for j in range(n)]
+        load_pieces.append(len(held))
+        for j in range(len(held)):
+            source[held[j]] = (i, j * PIECE_WORDS)
+
+    where = {}
+    for n in range(n_units):
+        for i in range(len(units[n])):
+            where[units[n][i]] = (n, i)
+    assert len(where) == len(source) == (GATES + BATCH_TILES) * N_PASSES
+
     passes = []
     for n in range(n_units):
-        if units[n][0] != Z:
-            passes.extend([(n, j) for j in range(W_UNIT_PASSES)])
+        for who, g in units[n]:
+            if who in range(GATES):
+                passes.append((who, g, max(n, where[((Z, 0), g)][0])))
+    assert len(passes) == GATES * N_PASSES
+    first_of_gate = {}
+    last_of_gate = {}
+    for i in range(len(passes)):
+        first_of_gate.setdefault(passes[i][0], i)
+        last_of_gate[passes[i][0]] = i
 
     with ExitStack() as stack:
         const = stack.enter_context(tc.tile_pool(name="const", bufs=1))
         raw_pool = stack.enter_context(tc.tile_pool(name="raw", bufs=RAW_BUFS))
-        grouped_pool = stack.enter_context(tc.tile_pool(name="grouped", bufs=3))
+        grouped_pool = stack.enter_context(tc.tile_pool(name="grouped", bufs=GROUPED_BUFS))
         mx_pool = stack.enter_context(tc.tile_pool(name="mx", bufs=MX_BUFS))
         cell = stack.enter_context(tc.tile_pool(name="cell", bufs=1))
         acc_pool = stack.enter_context(tc.psum_pool(name="acc", bufs=1))
-        ring = stack.enter_context(tc.psum_pool(name="ring", bufs=UNIT_BANKS))
+        ring = stack.enter_context(tc.psum_pool(name="ring", bufs=RING_BANKS))
         stack.enter_context(tc.manual_schedule())
 
         raw_tiles = {}
         grouped_tiles = {}
         mx_tiles = {}
+        banks_done = []
+        last_bank_of = {}
+        issued = []
+        last_burst = [0]
+        unread = list(load_pieces)
 
-        def load(n):
-            who, index = units[n]
-            raw = raw_pool.tile([P, UNIT_COLS], BF16)
-            raw_tiles[n] = raw
-            if who != Z:
-                nc.sync.dma_start(out=raw[:], in_=weights[who][:, index * W_UNIT_K : (index + 1) * W_UNIT_K])
-                return
-            first_k = index * Z_UNIT_K
-            by_batch_tile = raw[:].rearrange("p (m k) -> p m k", m=BATCH_TILES)
+        def burst(limit):
+            for count in range(limit):
+                i = len(issued)
+                if i == len(passes):
+                    return
+                unit = passes[i][2]
+                if unit not in last_bank_of:
+                    return
+                if last_bank_of[unit] + (LAG_BANKS * len(units[unit]) + MAX_PIECES - 1) // MAX_PIECES > len(banks_done):
+                    return
+                multiply(i)
+                issued.append(i)
+
+        def load_z(dest, rows, first_k, width):
             for part, part_k in z_parts:
                 lo = max(first_k, part_k)
-                hi = min(first_k + Z_UNIT_K, part_k + part.shape[1])
-                if lo < hi:
+                hi = min(first_k + width, part_k + part.shape[1])
+                if lo < hi and rows is None:
                     nc.sync.dma_start(
-                        out=by_batch_tile[:, :, lo - first_k : hi - first_k],
+                        out=dest[:, :, lo - first_k : hi - first_k],
                         in_=part[:, lo - part_k : hi - part_k].rearrange("(m p) k -> p m k", p=P),
                     )
+                elif lo < hi:
+                    nc.sync.dma_start(
+                        out=dest[:, lo - first_k : hi - first_k],
+                        in_=part[rows * P : (rows + 1) * P, lo - part_k : hi - part_k],
+                    )
+
+        def load(i):
+            spec = loads[i]
+            raw = raw_pool.tile([P, load_pieces[i] * PIECE_COLS], BF16, name="raw")
+            raw_tiles[i] = raw
+            if spec[0] == "zk":
+                kind, g0, n = spec
+                load_z(raw[:].rearrange("p (m k) -> p m k", m=BATCH_TILES), None, g0 * K_PASS, n * K_PASS)
+            elif spec[0] == "zm":
+                kind, m, g0, n = spec
+                load_z(raw, m, g0 * K_PASS, n * K_PASS)
+            else:
+                kind, gates, g0, n = spec
+                width = n * K_PASS
+                for j in range(len(gates)):
+                    nc.sync.dma_start(
+                        out=raw[:, j * width : (j + 1) * width],
+                        in_=weights[gates[j]][:, g0 * K_PASS : g0 * K_PASS + width],
+                    )
+
+        def load_more():
+            read = min([i for i in range(len(loads)) if unread[i] > 0] + [len(loads)])
+            for i in range(len(raw_tiles), min(len(loads), read + RAW_BUFS)):
+                load(i)
 
         def transpose_and_regroup(n):
-            words = raw_tiles[n][:].bitcast(F32)
-            if units[n][0] == Z:
-                pieces = words.rearrange("p (a b w) -> p b a w", a=BANK_PIECES, b=UNIT_BANKS)
-            else:
-                pieces = words.rearrange("p (b a w) -> p b a w", a=BANK_PIECES, b=UNIT_BANKS)
-            grouped = grouped_pool.tile([P, UNIT_COLS], BF16, align_bytes=64)
+            pieces = units[n]
+            n_banks = len(pieces) // BANK_PIECES
+            grouped = grouped_pool.tile([P, len(pieces) * PIECE_COLS], BF16, align_bytes=64, name="grouped")
             grouped_tiles[n] = grouped
             grouped_words = grouped[:].bitcast(F32).rearrange(
-                "p (b a r u) -> p b a r u", b=UNIT_BANKS, a=BANK_PIECES, u=2
+                "p (b a r u) -> p b a r u", b=n_banks, a=BANK_PIECES, u=2
             )
-            for b in range(UNIT_BANKS):
-                bank = ring.tile([P, BANK_PIECES, 2, P], F32)
+            for b in range(n_banks):
+                bank = ring.tile([P, BANK_PIECES, 2, P], F32, name="bank")
                 for a in range(BANK_PIECES):
+                    from_load, word = source[pieces[b * BANK_PIECES + a]]
+                    unread[from_load] -= 1
+                    words = raw_tiles[from_load][:].bitcast(F32)
                     for u in range(2):
                         nc.tensor.transpose(
-                            out=bank[:, a, u, :], in_=pieces[:, b, a, u * P : (u + 1) * P], identity=ident[:]
+                            out=bank[:, a, u, :], in_=words[:, word + u * P : word + (u + 1) * P], identity=ident[:]
                         )
                 joined = bank[:].rearrange("p a u r -> p a r u")
-                if b == VECTOR_BANK:
+                banks_done.append(n)
+                if len(banks_done) % VECTOR_EVERY == 0:
                     nc.vector.tensor_copy(out=grouped_words[:, b], in_=joined)
                 else:
                     nc.scalar.copy(out=grouped_words[:, b], in_=joined)
+                if b == n_banks - 1:
+                    last_bank_of[n] = len(banks_done)
+                if len(banks_done) - last_burst[-1] >= min(BURST_BANKS, n_banks):
+                    last_burst.append(len(banks_done))
+                    burst(BURST_PASSES)
 
         def quantise(n):
-            codes = mx_pool.tile([P, UNIT_CODES], U32, align_bytes=64)
-            scales = mx_pool.tile([P, UNIT_CODES], U8, align_bytes=64)
-            mx_tiles[units[n]] = (codes, scales)
-            nc.vector.quantize_mx(out=codes[:].bitcast(FP8X4), scales=scales[:], in_=grouped_tiles[n][:])
+            n_codes = len(units[n]) * P
+            codes = mx_pool.tile([P, n_codes], U32, align_bytes=64, name="codes")
+            scales = mx_pool.tile([P, n_codes], U8, align_bytes=64, name="scales")
+            mx_tiles[n] = (codes, scales)
+            step = min(QUANT_PIECES, len(units[n])) * P
+            for c in range(0, n_codes, step):
+                nc.vector.quantize_mx(
+                    out=codes[:, c : c + step].bitcast(FP8X4),
+                    scales=scales[:, c : c + step],
+                    in_=grouped_tiles[n][:, 4 * c : 4 * (c + step)],
+                )
 
-        def multiply(n, j):
-            gate, s = units[n]
-            w_codes, w_scales = mx_tiles[units[n]]
-            z_codes, z_scales = mx_tiles[(Z, Z_UNITS_PER_SET * s + j // Z_UNIT_PASSES)]
-            w_cols = slice(j * HIDDEN, (j + 1) * HIDDEN)
-            z_cols = slice((j % Z_UNIT_PASSES) * BATCH, (j % Z_UNIT_PASSES + 1) * BATCH)
+        def multiply(i):
+            gate, g, unit = passes[i]
+            w_unit_n, w_piece = where[(gate, g)]
+            z_unit_n, z_piece = where[((Z, 0), g)]
+            w_codes, w_scales = mx_tiles[w_unit_n]
+            z_codes, z_scales = mx_tiles[z_unit_n]
+            w_cols = slice(w_piece * P, (w_piece + 1) * P)
+            z_cols = slice(z_piece * P, z_piece * P + BATCH)
             nc.tensor.matmul_mx(
                 out=acc[gate][:],
                 lhsT=w_codes[:, w_cols].bitcast(FP8X4),
                 lhsT_scale=w_scales[:, w_cols],
                 rhs=z_codes[:, z_cols].bitcast(FP8X4),
                 rhs_scale=z_scales[:, z_cols],
-                start=(s == 0 and j == 0),
-                stop=(s == SETS - 1 and j == W_UNIT_PASSES - 1),
+                start=(first_of_gate[gate] == i),
+                stop=(last_of_gate[gate] == i),
             )
 
         old_rows = const.tile([P, BATCH_TILES, HIDDEN], BF16)
@@ -150,8 +257,7 @@ def tile_rnn_unit_k_kernel(
         nc.vector.memset(bias_rows[:], 0.0)
         for gate in range(GATES):
             nc.scalar.dma_start(out=bias_rows[gate : gate + 1, :], in_=biases[gate].unsqueeze(0))
-        for n in range(RAW_BUFS):
-            load(n)
+        load_more()
 
         dummy = const.tile([P, 1], F32)
         nc.vector.memset(dummy[:], 0.0)
@@ -170,28 +276,23 @@ def tile_rnn_unit_k_kernel(
             nc.vector.tensor_copy(out=old_rows_f32[:], in_=old_rows[:])
             bias_rows_f32 = const.tile([P, HIDDEN], F32)
             nc.vector.tensor_copy(out=bias_rows_f32[:], in_=bias_rows[:])
-            bank = ring.tile([P, BANK_PIECES, 2, P], F32)
+            bank = ring.tile([P, BANK_PIECES, 2, P], F32, name="bank")
             for m in range(BATCH_TILES):
                 nc.tensor.transpose(out=bank[:, 0, m, :], in_=old_rows_f32[:, m, :], identity=ident[:])
             nc.tensor.transpose(out=bank[:, 1, 0, :], in_=bias_rows_f32[:], identity=ident[:])
             nc.vector.tensor_copy(out=old_t[:], in_=bank[:, 0].rearrange("p m b -> p (m b)"))
             nc.vector.tensor_copy(out=bias_cols[:], in_=bank[:, 1, 0, 0:GATES])
 
-        issued = 0
-        for n in range(n_units + 1):
+        for n in range(n_units):
             if n >= 1:
                 quantise(n - 1)
-            if n < n_units:
-                transpose_and_regroup(n)
+            transpose_and_regroup(n)
             if n == 0:
                 prepare_cell_operands()
-            ready = len([p for p in passes if p[0] <= n - 2])
-            upto = min(ready, issued + PASSES_PER_UNIT) if n < n_units else len(passes)
-            for unit, j in passes[issued:upto]:
-                multiply(unit, j)
-            issued = upto
-            if n + RAW_BUFS < n_units:
-                load(n + RAW_BUFS)
+            load_more()
+        quantise(n_units - 1)
+        for i in range(len(issued), len(passes)):
+            multiply(i)
 
         def gate_value(gate, func, name):
             value = cell.tile([P, BATCH], F32, name=name)
@@ -217,7 +318,7 @@ def tile_rnn_unit_k_kernel(
 
         hidden = cell.tile([P, BATCH_TILES, HIDDEN], F32)
         for m in range(BATCH_TILES):
-            bank = ring.tile([P, BANK_PIECES, 2, P], F32)
+            bank = ring.tile([P, BANK_PIECES, 2, P], F32, name="bank")
             nc.tensor.transpose(out=bank[:, 0, 0, :], in_=hidden_t[:, m * P : (m + 1) * P], identity=ident[:])
             if m == 0:
                 nc.vector.tensor_copy(out=hidden[:, m, :], in_=bank[:, 0, 0, :])

@@ -32,7 +32,9 @@ VECTOR_EVERY = 4
 
 RAW_BUFS = 10
 GROUPED_BUFS = 3
-MX_BUFS = 13
+MX_BUFS = 6
+Z_BUFS = 3
+Z_SET = 8
 BURST_BANKS = 4
 BURST_PASSES = 6
 LAG_BANKS = 4
@@ -64,24 +66,23 @@ def tile_rnn_unit_k_kernel(
         return [(gate, g0 + j) for gate in gates for j in range(n)]
 
     SET = 8
-    HALF = SET // 2
     N_SETS = N_PASSES // SET
 
     def add(spec, pieces):
         loads.append(spec)
         units.append(pieces)
 
-    def add_z(s, h):
-        add(("zk", s * SET + h * HALF, HALF), z_pieces(s * SET + h * HALF, HALF))
+    def add_z(s, m):
+        add(("zm", m, s * SET, SET), [((Z, m), s * SET + j) for j in range(SET)])
 
     add_z(0, 0)
     add_z(0, 1)
     for s in range(N_SETS):
-        for h in range(2):
-            for gate in (2 * h, 2 * h + 1):
+        for m in range(BATCH_TILES):
+            for gate in (2 * m, 2 * m + 1):
                 add(("w", (gate,), s * SET, SET), w_pieces((gate,), s * SET, SET))
             if s + 1 < N_SETS:
-                add_z(s + 1, h)
+                add_z(s + 1, m)
     n_units = len(units)
 
     source = {}
@@ -107,11 +108,18 @@ def tile_rnn_unit_k_kernel(
             where[units[n][i]] = (n, i)
     assert len(where) == len(source) == (GATES + BATCH_TILES) * N_PASSES
 
+    place = {}
+    for who, g in where:
+        if who in range(GATES):
+            place[(who, g)] = (where[(who, g)][0], where[(who, g)][1] * P)
+        else:
+            place[(who, g)] = ((Z, g // Z_SET), ((g % Z_SET) * BATCH_TILES + who[1]) * P)
+
     passes = []
     for n in range(n_units):
         for who, g in units[n]:
             if who in range(GATES):
-                passes.append((who, g, max(n, where[((Z, 0), g)][0])))
+                passes.append((who, g, max([n] + [where[((Z, m), g)][0] for m in range(BATCH_TILES)])))
     assert len(passes) == GATES * N_PASSES
     first_of_gate = {}
     last_of_gate = {}
@@ -124,6 +132,7 @@ def tile_rnn_unit_k_kernel(
         raw_pool = stack.enter_context(tc.tile_pool(name="raw", bufs=RAW_BUFS))
         grouped_pool = stack.enter_context(tc.tile_pool(name="grouped", bufs=GROUPED_BUFS))
         mx_pool = stack.enter_context(tc.tile_pool(name="mx", bufs=MX_BUFS))
+        z_pool = stack.enter_context(tc.tile_pool(name="zmx", bufs=Z_BUFS))
         cell = stack.enter_context(tc.tile_pool(name="cell", bufs=1))
         acc_pool = stack.enter_context(tc.psum_pool(name="acc", bufs=1))
         ring = stack.enter_context(tc.psum_pool(name="ring", bufs=RING_BANKS))
@@ -221,26 +230,40 @@ def tile_rnn_unit_k_kernel(
                     burst(BURST_PASSES)
 
         def quantise(n):
-            n_codes = len(units[n]) * P
-            codes = mx_pool.tile([P, n_codes], U32, align_bytes=64, name="codes")
-            scales = mx_pool.tile([P, n_codes], U8, align_bytes=64, name="scales")
-            mx_tiles[n] = (codes, scales)
-            step = min(QUANT_PIECES, len(units[n])) * P
-            for c in range(0, n_codes, step):
+            pieces = units[n]
+            runs = []
+            for i in range(len(pieces)):
+                key, col = place[pieces[i]]
+                if runs and len(runs[-1]) < QUANT_PIECES and place[pieces[i - 1]] == (key, col - P):
+                    runs[-1].append(i)
+                else:
+                    runs.append([i])
+            for run in runs:
+                key, col = place[pieces[run[0]]]
+                if key not in mx_tiles and key == n:
+                    w_codes = mx_pool.tile([P, len(pieces) * P], U32, align_bytes=64, name="codes")
+                    w_scales = mx_pool.tile([P, len(pieces) * P], U8, align_bytes=64, name="scales")
+                    mx_tiles[key] = (w_codes, w_scales)
+                elif key not in mx_tiles:
+                    z_codes = z_pool.tile([P, Z_SET * BATCH], U32, align_bytes=64, name="z_codes")
+                    z_scales = z_pool.tile([P, Z_SET * BATCH], U8, align_bytes=64, name="z_scales")
+                    mx_tiles[key] = (z_codes, z_scales)
+                codes, scales = mx_tiles[key]
+                width = len(run) * P
                 nc.vector.quantize_mx(
-                    out=codes[:, c : c + step].bitcast(FP8X4),
-                    scales=scales[:, c : c + step],
-                    in_=grouped_tiles[n][:, 4 * c : 4 * (c + step)],
+                    out=codes[:, col : col + width].bitcast(FP8X4),
+                    scales=scales[:, col : col + width],
+                    in_=grouped_tiles[n][:, run[0] * PIECE_COLS : (run[0] + len(run)) * PIECE_COLS],
                 )
 
         def multiply(i):
             gate, g, unit = passes[i]
-            w_unit_n, w_piece = where[(gate, g)]
-            z_unit_n, z_piece = where[((Z, 0), g)]
-            w_codes, w_scales = mx_tiles[w_unit_n]
-            z_codes, z_scales = mx_tiles[z_unit_n]
-            w_cols = slice(w_piece * P, (w_piece + 1) * P)
-            z_cols = slice(z_piece * P, z_piece * P + BATCH)
+            w_key, w_col = place[(gate, g)]
+            z_key, z_col = place[((Z, 0), g)]
+            w_codes, w_scales = mx_tiles[w_key]
+            z_codes, z_scales = mx_tiles[z_key]
+            w_cols = slice(w_col, w_col + P)
+            z_cols = slice(z_col, z_col + BATCH)
             nc.tensor.matmul_mx(
                 out=acc[gate][:],
                 lhsT=w_codes[:, w_cols].bitcast(FP8X4),

@@ -317,34 +317,38 @@ def tile_rnn_unit_k_kernel(
         for i in range(len(issued), len(passes)):
             multiply(i)
 
-        def gate_value(gate, func, name):
-            value = cell.tile([P, BATCH], F32, name=name)
+        def gate_value(gate, func, name, cols):
+            value = cell.tile([P, cols.stop - cols.start], F32, name=name)
             nc.scalar.activation(
-                out=value[:], in_=acc[gate][:], func=func, bias=bias_cols[:, gate : gate + 1], scale=1.0
+                out=value[:], in_=acc[gate][:, cols], func=func, bias=bias_cols[:, gate : gate + 1], scale=1.0
             )
             return value
 
-        input_gate = gate_value(GATE_I, ACT.Sigmoid, "input_gate")
-        forget_gate = gate_value(GATE_F, ACT.Sigmoid, "forget_gate")
-        candidate = gate_value(GATE_S, ACT.Tanh, "candidate")
+        whole = slice(0, BATCH)
+        halves = [slice(m * P, (m + 1) * P) for m in range(BATCH_TILES)]
+        input_gate = gate_value(GATE_I, ACT.Sigmoid, "input_gate", whole)
+        forget_gate = gate_value(GATE_F, ACT.Sigmoid, "forget_gate", whole)
         kept = cell.tile([P, BATCH], F32)
         nc.vector.tensor_tensor(out=kept[:], in0=forget_gate[:], in1=old_t[:], op=ALU.mult)
-        added = cell.tile([P, BATCH], F32)
-        nc.vector.tensor_tensor(out=added[:], in0=input_gate[:], in1=candidate[:], op=ALU.mult)
-        new_state = cell.tile([P, BATCH], F32)
-        nc.vector.tensor_tensor(out=new_state[:], in0=kept[:], in1=added[:], op=ALU.add)
-        state_tanh = cell.tile([P, BATCH], F32)
-        nc.scalar.activation(out=state_tanh[:], in_=new_state[:], func=ACT.Tanh)
-        output_gate = gate_value(GATE_O, ACT.Sigmoid, "output_gate")
-        hidden_t = cell.tile([P, BATCH], F32)
-        nc.vector.tensor_tensor(out=hidden_t[:], in0=output_gate[:], in1=state_tanh[:], op=ALU.mult)
-
-        hidden = cell.tile([P, BATCH_TILES, HIDDEN], F32)
+        candidate = [gate_value(GATE_S, ACT.Tanh, "candidate%d" % m, halves[m]) for m in range(BATCH_TILES)]
+        state_tanh = []
         for m in range(BATCH_TILES):
+            added = cell.tile([P, P], F32, name="added%d" % m)
+            nc.vector.tensor_tensor(out=added[:], in0=input_gate[:, halves[m]], in1=candidate[m][:], op=ALU.mult)
+            new_state = cell.tile([P, P], F32, name="new_state%d" % m)
+            nc.vector.tensor_tensor(out=new_state[:], in0=kept[:, halves[m]], in1=added[:], op=ALU.add)
+            tanh_m = cell.tile([P, P], F32, name="state_tanh%d" % m)
+            nc.scalar.activation(out=tanh_m[:], in_=new_state[:], func=ACT.Tanh)
+            state_tanh.append(tanh_m)
+        hidden = cell.tile([P, BATCH_TILES, HIDDEN], F32)
+        banks = []
+        for m in range(BATCH_TILES):
+            output_gate = gate_value(GATE_O, ACT.Sigmoid, "output_gate%d" % m, halves[m])
+            hidden_t = cell.tile([P, P], F32, name="hidden_t%d" % m)
+            nc.vector.tensor_tensor(out=hidden_t[:], in0=output_gate[:], in1=state_tanh[m][:], op=ALU.mult)
             bank = ring.tile([P, BANK_PIECES, 2, P], F32, name="bank")
-            nc.tensor.transpose(out=bank[:, 0, 0, :], in_=hidden_t[:, m * P : (m + 1) * P], identity=ident[:])
-            if m == 0:
-                nc.vector.tensor_copy(out=hidden[:, m, :], in_=bank[:, 0, 0, :])
-            else:
-                nc.scalar.copy(out=hidden[:, m, :], in_=bank[:, 0, 0, :])
+            nc.tensor.transpose(out=bank[:, 0, 0, :], in_=hidden_t[:], identity=ident[:])
+            banks.append(bank)
+        nc.scalar.copy(out=hidden[:, 0, :], in_=banks[0][:, 0, 0, :])
+        nc.vector.tensor_copy(out=hidden[:, 1, :], in_=banks[1][:, 0, 0, :])
         nc.sync.dma_start(out=out.rearrange("(m p) h -> p m h", p=P), in_=hidden[:])

@@ -350,5 +350,6 @@ def tile_rnn_unit_k_kernel(
             nc.tensor.transpose(out=bank[:, 0, 0, :], in_=hidden_t[:], identity=ident[:])
             banks.append(bank)
         nc.scalar.copy(out=hidden[:, 0, :], in_=banks[0][:, 0, 0, :])
+        nc.scalar.dma_start(out=out[0:P, :], in_=hidden[:, 0, :])
         nc.vector.tensor_copy(out=hidden[:, 1, :], in_=banks[1][:, 0, 0, :])
-        nc.sync.dma_start(out=out.rearrange("(m p) h -> p m h", p=P), in_=hidden[:])
+        nc.sync.dma_start(out=out[P : 2 * P, :], in_=hidden[:, 1, :])

from contextlib import ExitStack

import concourse.mybir as mybir
from concourse.masks import make_identity

BF16 = mybir.dt.bfloat16
F32 = mybir.dt.float32
U32 = mybir.dt.uint32
U8 = mybir.dt.uint8
FP8X4 = mybir.dt.float8_e4m3fn_x4
ACT = mybir.ActivationFunctionType
ALU = mybir.AluOpType

P = 128
BATCH = 256
BATCH_TILES = BATCH // P
HIDDEN = 128
K = 16384
K_PASS = 512
N_PASSES = K // K_PASS
GATES = 4
Z = "z"

FLOPS = 2 * BATCH * GATES * HIDDEN * K

PIECE_COLS = K_PASS
PIECE_WORDS = PIECE_COLS // 2
BANK_PIECES = 2
MAX_PIECES = 8
RING_BANKS = 4
VECTOR_EVERY = 4

RAW_BUFS = 10
GROUPED_BUFS = 3
MX_BUFS = 6
Z_BUFS = 3
Z_SET = 8
BURST_BANKS = 4
BURST_PASSES = 6
LAG_BANKS = 4
QUANT_PIECES = 4


def tile_rnn_unit_k_kernel(
    tc, input_x, previous_time, previous_layer, old_state, Wi, bi, Wf, bf, Wo, bo, Ws, bs_state, out
):
    nc = tc.nc

    weights = [Wi, Wf, Ws, Wo]
    biases = [bi, bf, bs_state, bo]
    GATE_I, GATE_F, GATE_S, GATE_O = 0, 1, 2, 3

    z_parts = [
        (input_x, 0),
        (previous_time, input_x.shape[1]),
        (previous_layer, input_x.shape[1] + previous_time.shape[1]),
    ]

    loads = []
    units = []

    def z_pieces(g0, n):
        return [((Z, m), g0 + j) for j in range(n) for m in range(BATCH_TILES)]

    def w_pieces(gates, g0, n):
        return [(gate, g0 + j) for gate in gates for j in range(n)]

    SET = 8
    N_SETS = N_PASSES // SET

    def add(spec, pieces):
        loads.append(spec)
        units.append(pieces)

    def add_z(s, m):
        add(("zm", m, s * SET, SET), [((Z, m), s * SET + j) for j in range(SET)])

    add_z(0, 0)
    add_z(0, 1)
    for s in range(N_SETS):
        for m in range(BATCH_TILES):
            for gate in (2 * m, 2 * m + 1):
                add(("w", (gate,), s * SET, SET), w_pieces((gate,), s * SET, SET))
            if s + 1 < N_SETS:
                add_z(s + 1, m)
    n_units = len(units)

    source = {}
    load_pieces = []
    for i in range(len(loads)):
        spec = loads[i]
        if spec[0] == "zk":
            kind, g0, n = spec
            held = [((Z, m), g0 + j) for m in range(BATCH_TILES) for j in range(n)]
        elif spec[0] == "zm":
            kind, m, g0, n = spec
            held = [((Z, m), g0 + j) for j in range(n)]
        else:
            kind, gates, g0, n = spec
            held = [(gate, g0 + j) for gate in gates for j in range(n)]
        load_pieces.append(len(held))
        for j in range(len(held)):
            source[held[j]] = (i, j * PIECE_WORDS)

    where = {}
    for n in range(n_units):
        for i in range(len(units[n])):
            where[units[n][i]] = (n, i)
    assert len(where) == len(source) == (GATES + BATCH_TILES) * N_PASSES

    place = {}
    for who, g in where:
        if who in range(GATES):
            place[(who, g)] = (where[(who, g)][0], where[(who, g)][1] * P)
        else:
            place[(who, g)] = ((Z, g // Z_SET), ((g % Z_SET) * BATCH_TILES + who[1]) * P)

    passes = []
    for n in range(n_units):
        for who, g in units[n]:
            if who in range(GATES):
                passes.append((who, g, max([n] + [where[((Z, m), g)][0] for m in range(BATCH_TILES)])))
    assert len(passes) == GATES * N_PASSES
    first_of_gate = {}
    last_of_gate = {}
    for i in range(len(passes)):
        first_of_gate.setdefault(passes[i][0], i)
        last_of_gate[passes[i][0]] = i

    with ExitStack() as stack:
        const = stack.enter_context(tc.tile_pool(name="const", bufs=1))
        raw_pool = stack.enter_context(tc.tile_pool(name="raw", bufs=RAW_BUFS))
        grouped_pool = stack.enter_context(tc.tile_pool(name="grouped", bufs=GROUPED_BUFS))
        mx_pool = stack.enter_context(tc.tile_pool(name="mx", bufs=MX_BUFS))
        z_pool = stack.enter_context(tc.tile_pool(name="zmx", bufs=Z_BUFS))
        cell = stack.enter_context(tc.tile_pool(name="cell", bufs=1))
        acc_pool = stack.enter_context(tc.psum_pool(name="acc", bufs=1))
        ring = stack.enter_context(tc.psum_pool(name="ring", bufs=RING_BANKS))
        stack.enter_context(tc.manual_schedule())

        raw_tiles = {}
        grouped_tiles = {}
        mx_tiles = {}
        banks_done = []
        last_bank_of = {}
        issued = []
        last_burst = [0]
        unread = list(load_pieces)

        def burst(limit):
            for count in range(limit):
                i = len(issued)
                if i == len(passes):
                    return
                unit = passes[i][2]
                if unit not in last_bank_of:
                    return
                if last_bank_of[unit] + (LAG_BANKS * len(units[unit]) + MAX_PIECES - 1) // MAX_PIECES > len(banks_done):
                    return
                multiply(i)
                issued.append(i)

        def load_z(dest, rows, first_k, width):
            for part, part_k in z_parts:
                lo = max(first_k, part_k)
                hi = min(first_k + width, part_k + part.shape[1])
                if lo < hi and rows is None:
                    nc.sync.dma_start(
                        out=dest[:, :, lo - first_k : hi - first_k],
                        in_=part[:, lo - part_k : hi - part_k].rearrange("(m p) k -> p m k", p=P),
                    )
                elif lo < hi:
                    nc.sync.dma_start(
                        out=dest[:, lo - first_k : hi - first_k],
                        in_=part[rows * P : (rows + 1) * P, lo - part_k : hi - part_k],
                    )

        def load(i):
            spec = loads[i]
            raw = raw_pool.tile([P, load_pieces[i] * PIECE_COLS], BF16, name="raw")
            raw_tiles[i] = raw
            if spec[0] == "zk":
                kind, g0, n = spec
                load_z(raw[:].rearrange("p (m k) -> p m k", m=BATCH_TILES), None, g0 * K_PASS, n * K_PASS)
            elif spec[0] == "zm":
                kind, m, g0, n = spec
                load_z(raw, m, g0 * K_PASS, n * K_PASS)
            else:
                kind, gates, g0, n = spec
                width = n * K_PASS
                for j in range(len(gates)):
                    nc.sync.dma_start(
                        out=raw[:, j * width : (j + 1) * width],
                        in_=weights[gates[j]][:, g0 * K_PASS : g0 * K_PASS + width],
                    )

        def load_more():
            read = min([i for i in range(len(loads)) if unread[i] > 0] + [len(loads)])
            for i in range(len(raw_tiles), min(len(loads), read + RAW_BUFS)):
                load(i)

        def transpose_and_regroup(n):
            pieces = units[n]
            n_banks = len(pieces) // BANK_PIECES
            grouped = grouped_pool.tile([P, len(pieces) * PIECE_COLS], BF16, align_bytes=64, name="grouped")
            grouped_tiles[n] = grouped
            grouped_words = grouped[:].bitcast(F32).rearrange(
                "p (b a r u) -> p b a r u", b=n_banks, a=BANK_PIECES, u=2
            )
            for b in range(n_banks):
                bank = ring.tile([P, BANK_PIECES, 2, P], F32, name="bank")
                for a in range(BANK_PIECES):
                    from_load, word = source[pieces[b * BANK_PIECES + a]]
                    unread[from_load] -= 1
                    words = raw_tiles[from_load][:].bitcast(F32)
                    for u in range(2):
                        nc.tensor.transpose(
                            out=bank[:, a, u, :], in_=words[:, word + u * P : word + (u + 1) * P], identity=ident[:]
                        )
                joined = bank[:].rearrange("p a u r -> p a r u")
                banks_done.append(n)
                if len(banks_done) % VECTOR_EVERY == 0:
                    nc.vector.tensor_copy(out=grouped_words[:, b], in_=joined)
                else:
                    nc.scalar.copy(out=grouped_words[:, b], in_=joined)
                if b == n_banks - 1:
                    last_bank_of[n] = len(banks_done)
                if len(banks_done) - last_burst[-1] >= min(BURST_BANKS, n_banks):
                    last_burst.append(len(banks_done))
                    burst(BURST_PASSES)

        def quantise(n):
            pieces = units[n]
            runs = []
            for i in range(len(pieces)):
                key, col = place[pieces[i]]
                if runs and len(runs[-1]) < QUANT_PIECES and place[pieces[i - 1]] == (key, col - P):
                    runs[-1].append(i)
                else:
                    runs.append([i])
            for run in runs:
                key, col = place[pieces[run[0]]]
                if key not in mx_tiles and key == n:
                    w_codes = mx_pool.tile([P, len(pieces) * P], U32, align_bytes=64, name="codes")
                    w_scales = mx_pool.tile([P, len(pieces) * P], U8, align_bytes=64, name="scales")
                    mx_tiles[key] = (w_codes, w_scales)
                elif key not in mx_tiles:
                    z_codes = z_pool.tile([P, Z_SET * BATCH], U32, align_bytes=64, name="z_codes")
                    z_scales = z_pool.tile([P, Z_SET * BATCH], U8, align_bytes=64, name="z_scales")
                    mx_tiles[key] = (z_codes, z_scales)
                codes, scales = mx_tiles[key]
                width = len(run) * P
                nc.vector.quantize_mx(
                    out=codes[:, col : col + width].bitcast(FP8X4),
                    scales=scales[:, col : col + width],
                    in_=grouped_tiles[n][:, run[0] * PIECE_COLS : (run[0] + len(run)) * PIECE_COLS],
                )

        def multiply(i):
            gate, g, unit = passes[i]
            w_key, w_col = place[(gate, g)]
            z_key, z_col = place[((Z, 0), g)]
            w_codes, w_scales = mx_tiles[w_key]
            z_codes, z_scales = mx_tiles[z_key]
            w_cols = slice(w_col, w_col + P)
            z_cols = slice(z_col, z_col + BATCH)
            nc.tensor.matmul_mx(
                out=acc[gate][:],
                lhsT=w_codes[:, w_cols].bitcast(FP8X4),
                lhsT_scale=w_scales[:, w_cols],
                rhs=z_codes[:, z_cols].bitcast(FP8X4),
                rhs_scale=z_scales[:, z_cols],
                start=(first_of_gate[gate] == i),
                stop=(last_of_gate[gate] == i),
            )

        old_rows = const.tile([P, BATCH_TILES, HIDDEN], BF16)
        nc.scalar.dma_start(out=old_rows[:], in_=old_state.rearrange("(m p) h -> p m h", p=P))
        bias_rows = const.tile([P, HIDDEN], BF16)
        nc.vector.memset(bias_rows[:], 0.0)
        for gate in range(GATES):
            nc.scalar.dma_start(out=bias_rows[gate : gate + 1, :], in_=biases[gate].unsqueeze(0))
        load_more()

        dummy = const.tile([P, 1], F32)
        nc.vector.memset(dummy[:], 0.0)
        nc.scalar.activation(out=dummy[:], in_=dummy[:], func=ACT.Sigmoid)

        ident = const.tile([P, P], F32)
        make_identity(nc, ident[:])

        acc = [acc_pool.tile([P, BATCH], F32, name="acc%d" % gate) for gate in range(GATES)]

        old_t = const.tile([P, BATCH], F32)
        bias_cols = const.tile([P, GATES], F32)

        def prepare_cell_operands():
            old_rows_f32 = const.tile([P, BATCH_TILES, HIDDEN], F32)
            nc.vector.tensor_copy(out=old_rows_f32[:], in_=old_rows[:])
            bias_rows_f32 = const.tile([P, HIDDEN], F32)
            nc.vector.tensor_copy(out=bias_rows_f32[:], in_=bias_rows[:])
            bank = ring.tile([P, BANK_PIECES, 2, P], F32, name="bank")
            for m in range(BATCH_TILES):
                nc.tensor.transpose(out=bank[:, 0, m, :], in_=old_rows_f32[:, m, :], identity=ident[:])
            nc.tensor.transpose(out=bank[:, 1, 0, :], in_=bias_rows_f32[:], identity=ident[:])
            nc.vector.tensor_copy(out=old_t[:], in_=bank[:, 0].rearrange("p m b -> p (m b)"))
            nc.vector.tensor_copy(out=bias_cols[:], in_=bank[:, 1, 0, 0:GATES])

        for n in range(n_units):
            if n >= 1:
                quantise(n - 1)
            transpose_and_regroup(n)
            if n == 0:
                prepare_cell_operands()
            load_more()
        quantise(n_units - 1)
        for i in range(len(issued), len(passes)):
            multiply(i)

        def gate_value(gate, func, name, cols):
            value = cell.tile([P, cols.stop - cols.start], F32, name=name)
            nc.scalar.activation(
                out=value[:], in_=acc[gate][:, cols], func=func, bias=bias_cols[:, gate : gate + 1], scale=1.0
            )
            return value

        whole = slice(0, BATCH)
        halves = [slice(m * P, (m + 1) * P) for m in range(BATCH_TILES)]
        input_gate = gate_value(GATE_I, ACT.Sigmoid, "input_gate", whole)
        forget_gate = gate_value(GATE_F, ACT.Sigmoid, "forget_gate", whole)
        kept = cell.tile([P, BATCH], F32)
        nc.vector.tensor_tensor(out=kept[:], in0=forget_gate[:], in1=old_t[:], op=ALU.mult)
        candidate = [gate_value(GATE_S, ACT.Tanh, "candidate%d" % m, halves[m]) for m in range(BATCH_TILES)]
        state_tanh = []
        for m in range(BATCH_TILES):
            added = cell.tile([P, P], F32, name="added%d" % m)
            nc.vector.tensor_tensor(out=added[:], in0=input_gate[:, halves[m]], in1=candidate[m][:], op=ALU.mult)
            new_state = cell.tile([P, P], F32, name="new_state%d" % m)
            nc.vector.tensor_tensor(out=new_state[:], in0=kept[:, halves[m]], in1=added[:], op=ALU.add)
            tanh_m = cell.tile([P, P], F32, name="state_tanh%d" % m)
            nc.scalar.activation(out=tanh_m[:], in_=new_state[:], func=ACT.Tanh)
            state_tanh.append(tanh_m)
        hidden = cell.tile([P, BATCH_TILES, HIDDEN], F32)
        banks = []
        for m in range(BATCH_TILES):
            output_gate = gate_value(GATE_O, ACT.Sigmoid, "output_gate%d" % m, halves[m])
            hidden_t = cell.tile([P, P], F32, name="hidden_t%d" % m)
            nc.vector.tensor_tensor(out=hidden_t[:], in0=output_gate[:], in1=state_tanh[m][:], op=ALU.mult)
            bank = ring.tile([P, BANK_PIECES, 2, P], F32, name="bank")
            nc.tensor.transpose(out=bank[:, 0, 0, :], in_=hidden_t[:], identity=ident[:])
            banks.append(bank)
        nc.scalar.copy(out=hidden[:, 0, :], in_=banks[0][:, 0, 0, :])
        nc.scalar.dma_start(out=out[0:P, :], in_=hidden[:, 0, :])
        nc.vector.tensor_copy(out=hidden[:, 1, :], in_=banks[1][:, 0, 0, :])
        nc.sync.dma_start(out=out[P : 2 * P, :], in_=hidden[:, 1, :])
